import numpy as np
import ml_dtypes

BF16 = ml_dtypes.bfloat16


def bf(x):
    return np.asarray(x, np.float32).astype(BF16)


def f32(x):
    return np.asarray(x, np.float32)


def f64(x):
    return np.asarray(x).astype(np.float64)


def striped(idx):
    return np.tile(idx.reshape(-1, 16).T, (8, 1))


C, HALF, S, N = 256, 128, 4096, 512
EPS = 1e-5


def setup_inputs():
    theta = np.random.uniform(0.0, 2.0 * np.pi, (HALF, N))
    return {"base": f32(np.random.standard_normal((C, S))), "x": f32(np.random.standard_normal((C, N))), "ln_w": f32(1.0 + 0.1 * np.random.standard_normal((C, 1))), "ln_b": f32(0.1 * np.random.standard_normal((C, 1))), "w": bf(np.random.standard_normal((C, C)) / np.sqrt(C)), "b": f32(0.2 * np.random.standard_normal((C, 1))), "cos_pos": f32(np.cos(theta)), "sin_pos": f32(np.sin(theta)), "offs": striped(np.random.permutation(S)[:N])}


def reference(base, x, ln_w, ln_b, w, b, cos_pos, sin_pos, offs):
    idx = offs[:16].T.reshape(-1)
    xx = f64(x)
    mean = xx.mean(axis=0, keepdims=True)
    var = np.square(xx - mean).mean(axis=0, keepdims=True)
    xn = (xx - mean) / np.sqrt(var + EPS) * f64(ln_w) + f64(ln_b)
    t = f64(w).T @ xn + f64(b)
    te, to = t[:HALF], t[HALF:]
    co, si = f64(cos_pos), f64(sin_pos)
    out = f64(base).copy()
    out[:HALF, idx] = te * co + (-to) * si
    out[HALF:, idx] = to * co + te * si
    return out

@@ -1,0 +1,96 @@
+import concourse.mybir as mybir
+
+F32, BF16, U16 = mybir.dt.float32, mybir.dt.bfloat16, mybir.dt.uint16
+ADD, SUBTRACT, MULT = mybir.AluOpType.add, mybir.AluOpType.subtract, mybir.AluOpType.mult
+ACT = mybir.ActivationFunctionType
+
+P = 128
+C = 256
+BLOCKS = C // P
+S = 4096
+N = 512
+EPS = 1e-5
+
+FLOPS = 2 * C * C * N
+
+
+def tile_gptj_cloud_kernel(tc, base, x, ln_w, ln_b, w, b, cos_pos, sin_pos, offs, out):
+    nc = tc.nc
+    with (
+        tc.tile_pool(name="held", bufs=1) as held,
+        tc.psum_pool(name="psum", bufs=1) as psum,
+    ):
+        offsets = held.tile([P, N // 16], U16, name="offsets")
+        nc.sync.dma_start(offsets[:], offs)
+
+        x_blk = [held.tile([P, N], F32, name=f"x{k}") for k in range(BLOCKS)]
+        for k in range(BLOCKS):
+            nc.sync.dma_start(x_blk[k][:], x[k * P : (k + 1) * P, :])
+
+        gain = held.tile([P, BLOCKS], F32, name="gain")
+        shift = held.tile([P, BLOCKS], F32, name="shift")
+        bias = held.tile([P, BLOCKS], F32, name="bias")
+        with nc.allow_non_contiguous_dma(reason="256 floats, one to a partition"):
+            for vec_tile, vec in ((gain, ln_w), (shift, ln_b), (bias, b)):
+                nc.gpsimd.dma_start(vec_tile[:], vec.rearrange("(k p) o -> p (k o)", p=P))
+
+        w_sb = held.tile([P, BLOCKS, C], BF16, name="w_sb")
+        nc.scalar.dma_start(w_sb[:], w.rearrange("(k p) c -> p k c", p=P))
+        cos_sb = held.tile([P, N], F32, name="cos_sb")
+        nc.scalar.dma_start(cos_sb[:], cos_pos)
+        sin_sb = held.tile([P, N], F32, name="sin_sb")
+        nc.scalar.dma_start(sin_sb[:], sin_pos)
+
+        window = [held.tile([P, S], F32, name=f"window{h}") for h in range(BLOCKS)]
+        for h in range(BLOCKS):
+            nc.sync.dma_start(window[h][:], base[h * P : (h + 1) * P, :])
+
+        averager = held.tile([P, P], F32, name="averager")
+        nc.gpsimd.memset(averager[:], 1.0 / C)
+        eps = held.tile([P, 1], F32, name="eps")
+        nc.gpsimd.memset(eps[:], EPS)
+        minus_sin = held.tile([P, N], F32, name="minus_sin")
+        nc.gpsimd.tensor_scalar_mul(minus_sin[:], sin_sb[:], -1.0)
+
+        mean = psum.tile([P, N], F32, name="mean")
+        for k in range(BLOCKS):
+            nc.tensor.matmul(mean[:], averager[:], x_blk[k][:], start=(k == 0), stop=(k == BLOCKS - 1))
+
+        centred = [held.tile([P, N], F32, name=f"centred{k}") for k in range(BLOCKS)]
+        squared = [held.tile([P, N], F32, name=f"squared{k}") for k in range(BLOCKS)]
+        for k in range(BLOCKS):
+            nc.vector.tensor_tensor(centred[k][:], x_blk[k][:], mean[:], SUBTRACT)
+            nc.scalar.activation(squared[k][:], centred[k][:], ACT.Square)
+
+        var = psum.tile([P, N], F32, name="var")
+        for k in range(BLOCKS):
+            nc.tensor.matmul(var[:], averager[:], squared[k][:], start=(k == 0), stop=(k == BLOCKS - 1))
+
+        rstd = held.tile([P, N], F32, name="rstd")
+        nc.scalar.activation(rstd[:], var[:], ACT.Abs_reciprocal_sqrt, bias=eps[:, 0:1])
+
+        unit = [held.tile([P, N], F32, name=f"unit{k}") for k in range(BLOCKS)]
+        xn = [held.tile([P, N], BF16, name=f"xn{k}") for k in range(BLOCKS)]
+        for k in range(BLOCKS):
+            nc.vector.tensor_tensor(unit[k][:], centred[k][:], rstd[:], MULT)
+            nc.scalar.activation(
+                xn[k][:], unit[k][:], ACT.Identity, bias=shift[:, k : k + 1], scale=gain[:, k : k + 1]
+            )
+
+        t = [psum.tile([P, N], F32, name=f"t{h}") for h in range(BLOCKS)]
+        for k in range(BLOCKS):
+            for h in range(BLOCKS):
+                nc.tensor.matmul(
+                    t[h][:], w_sb[:, k, h * P : (h + 1) * P], xn[k][:], start=(k == 0), stop=(k == BLOCKS - 1)
+                )
+
+        for h, partner_factor in ((0, minus_sin), (1, sin_sb)):
+            partner = 1 - h
+            own = held.tile([P, N], F32, name=f"own{h}")
+            nc.vector.scalar_tensor_tensor(own[:], t[h][:], bias[:, h : h + 1], cos_sb[:], ADD, MULT)
+            cross = held.tile([P, N], F32, name=f"cross{h}")
+            nc.vector.scalar_tensor_tensor(
+                cross[:], t[partner][:], bias[:, partner : partner + 1], partner_factor[:], ADD, MULT
+            )
+            nc.vector.tensor_tensor(window[h][:].indirect(offsets[:]), own[:], cross[:], ADD)
+            nc.sync.dma_start(out[h * P : (h + 1) * P, :], window[h][:])

@@ -9,88 +9,121 @@ C = 256
 BLOCKS = C // P
 S = 4096
 N = 512
+CHUNKS = 2
+T = N // CHUNKS
 EPS = 1e-5
+WARMING_MATMULS = 6
 
 FLOPS = 2 * C * C * N
 
 
 def tile_gptj_cloud_kernel(tc, base, x, ln_w, ln_b, w, b, cos_pos, sin_pos, offs, out):
     nc = tc.nc
+    blocks = range(BLOCKS)
+    chunks = range(CHUNKS)
+    cols = [slice(c * T, (c + 1) * T) for c in chunks]
+    rows = [slice(k * P, (k + 1) * P) for k in blocks]
     with (
         tc.tile_pool(name="held", bufs=1) as held,
         tc.psum_pool(name="psum", bufs=1) as psum,
     ):
-        offsets = held.tile([P, N // 16], U16, name="offsets")
-        nc.sync.dma_start(offsets[:], offs)
-
-        x_blk = [held.tile([P, N], F32, name=f"x{k}") for k in range(BLOCKS)]
-        for k in range(BLOCKS):
-            nc.sync.dma_start(x_blk[k][:], x[k * P : (k + 1) * P, :])
+        x_sb = held.tile([P, BLOCKS, N], F32, name="x_sb")
+        x_blk = [x_sb[:, k, :] for k in blocks]
+        for c in chunks:
+            nc.sync.dma_start(x_sb[:, :, cols[c]], x[:, cols[c]].rearrange("(k p) n -> p k n", p=P))
 
         gain = held.tile([P, BLOCKS], F32, name="gain")
         shift = held.tile([P, BLOCKS], F32, name="shift")
         bias = held.tile([P, BLOCKS], F32, name="bias")
-        with nc.allow_non_contiguous_dma(reason="256 floats, one to a partition"):
-            for vec_tile, vec in ((gain, ln_w), (shift, ln_b), (bias, b)):
-                nc.gpsimd.dma_start(vec_tile[:], vec.rearrange("(k p) o -> p (k o)", p=P))
-
         w_sb = held.tile([P, BLOCKS, C], BF16, name="w_sb")
-        nc.scalar.dma_start(w_sb[:], w.rearrange("(k p) c -> p k c", p=P))
-        cos_sb = held.tile([P, N], F32, name="cos_sb")
-        nc.scalar.dma_start(cos_sb[:], cos_pos)
         sin_sb = held.tile([P, N], F32, name="sin_sb")
-        nc.scalar.dma_start(sin_sb[:], sin_pos)
+        cos_sb = held.tile([P, N], F32, name="cos_sb")
+        offsets = held.tile([P, N // 16], U16, name="offsets")
+        window = [held.tile([P, S], F32, name=f"window{h}") for h in blocks]
 
-        window = [held.tile([P, S], F32, name=f"window{h}") for h in range(BLOCKS)]
-        for h in range(BLOCKS):
-            nc.sync.dma_start(window[h][:], base[h * P : (h + 1) * P, :])
+        with nc.allow_non_contiguous_dma(reason="256 floats, one to a partition"):
+            nc.sync.dma_start(gain[:], ln_w.rearrange("(k p) o -> p (k o)", p=P))
+            nc.sync.dma_start(shift[:], ln_b.rearrange("(k p) o -> p (k o)", p=P))
+        nc.sync.dma_start(w_sb[:], w.rearrange("(k p) c -> p k c", p=P))
+        nc.sync.dma_start(sin_sb[:], sin_pos)
+        nc.sync.dma_start(cos_sb[:], cos_pos)
+        nc.sync.dma_start(window[0][:], base[rows[0], :])
+        with nc.allow_non_contiguous_dma(reason="256 floats, one to a partition"):
+            nc.sync.dma_start(bias[:], b.rearrange("(k p) o -> p (k o)", p=P))
+        nc.sync.dma_start(offsets[:], offs)
+        nc.sync.dma_start(window[1][:], base[rows[1], :])
 
         averager = held.tile([P, P], F32, name="averager")
-        nc.gpsimd.memset(averager[:], 1.0 / C)
+        nc.vector.memset(averager[:], 1.0 / C)
         eps = held.tile([P, 1], F32, name="eps")
-        nc.gpsimd.memset(eps[:], EPS)
+        nc.vector.memset(eps[:], EPS)
         minus_sin = held.tile([P, N], F32, name="minus_sin")
-        nc.gpsimd.tensor_scalar_mul(minus_sin[:], sin_sb[:], -1.0)
+        nc.gpsimd.tensor_scalar(minus_sin[:], sin_sb[:], -1.0, 0.0, MULT, ADD)
 
-        mean = psum.tile([P, N], F32, name="mean")
-        for k in range(BLOCKS):
-            nc.tensor.matmul(mean[:], averager[:], x_blk[k][:], start=(k == 0), stop=(k == BLOCKS - 1))
+        table_warmer = held.tile([P, 1], F32, name="table_warmer")
+        nc.scalar.activation(table_warmer[:], eps[:], ACT.Abs_reciprocal_sqrt)
+        zeros = held.tile([P, N], BF16, name="zeros")
+        nc.gpsimd.memset(zeros[:], 0.0)
+        clock_warmer = psum.tile([P, N], F32, name="clock_warmer", tag="stat", bufs=4)
+        for i in range(WARMING_MATMULS):
+            nc.tensor.matmul(clock_warmer[:], zeros[:, 0:P], zeros[:], start=True, stop=True)
 
-        centred = [held.tile([P, N], F32, name=f"centred{k}") for k in range(BLOCKS)]
-        squared = [held.tile([P, N], F32, name=f"squared{k}") for k in range(BLOCKS)]
-        for k in range(BLOCKS):
-            nc.vector.tensor_tensor(centred[k][:], x_blk[k][:], mean[:], SUBTRACT)
-            nc.scalar.activation(squared[k][:], centred[k][:], ACT.Square)
+        x_sum = held.tile([P, N], F32, name="x_sum")
+        mean = [psum.tile([P, T], F32, name=f"mean{c}", tag="stat", bufs=4) for c in chunks]
+        for c in chunks:
+            nc.vector.tensor_tensor(x_sum[:, cols[c]], x_blk[0][:, cols[c]], x_blk[1][:, cols[c]], ADD)
+            nc.tensor.matmul(mean[c][:], averager[:], x_sum[:, cols[c]], start=True, stop=True)
 
-        var = psum.tile([P, N], F32, name="var")
-        for k in range(BLOCKS):
-            nc.tensor.matmul(var[:], averager[:], squared[k][:], start=(k == 0), stop=(k == BLOCKS - 1))
+        centred = [held.tile([P, N], F32, name=f"centred{k}") for k in blocks]
+        squared = [held.tile([P, N], F32, name=f"squared{k}") for k in blocks]
+        var = [psum.tile([P, T], F32, name=f"var{c}", tag="stat", bufs=4) for c in chunks]
+        for c in chunks:
+            for k in blocks:
+                nc.vector.tensor_tensor(centred[k][:, cols[c]], x_blk[k][:, cols[c]], mean[c][:], SUBTRACT)
+                nc.scalar.activation(squared[k][:, cols[c]], centred[k][:, cols[c]], ACT.Square)
+                nc.tensor.matmul(
+                    var[c][:], averager[:], squared[k][:, cols[c]], start=(k == 0), stop=(k == BLOCKS - 1)
+                )
 
         rstd = held.tile([P, N], F32, name="rstd")
-        nc.scalar.activation(rstd[:], var[:], ACT.Abs_reciprocal_sqrt, bias=eps[:, 0:1])
-
-        unit = [held.tile([P, N], F32, name=f"unit{k}") for k in range(BLOCKS)]
-        xn = [held.tile([P, N], BF16, name=f"xn{k}") for k in range(BLOCKS)]
-        for k in range(BLOCKS):
-            nc.vector.tensor_tensor(unit[k][:], centred[k][:], rstd[:], MULT)
-            nc.scalar.activation(
-                xn[k][:], unit[k][:], ACT.Identity, bias=shift[:, k : k + 1], scale=gain[:, k : k + 1]
-            )
-
-        t = [psum.tile([P, N], F32, name=f"t{h}") for h in range(BLOCKS)]
-        for k in range(BLOCKS):
-            for h in range(BLOCKS):
-                nc.tensor.matmul(
-                    t[h][:], w_sb[:, k, h * P : (h + 1) * P], xn[k][:], start=(k == 0), stop=(k == BLOCKS - 1)
+        unit = [held.tile([P, N], F32, name=f"unit{k}") for k in blocks]
+        xn = [held.tile([P, N], BF16, name=f"xn{k}") for k in blocks]
+        t = [[psum.tile([P, T], F32, name=f"t{h}{c}") for c in chunks] for h in blocks]
+        for c in chunks:
+            nc.scalar.activation(rstd[:, cols[c]], var[c][:], ACT.Abs_reciprocal_sqrt, bias=eps[:, 0:1])
+            for k in blocks:
+                nc.vector.tensor_tensor(unit[k][:, cols[c]], centred[k][:, cols[c]], rstd[:, cols[c]], MULT)
+                nc.scalar.activation(
+                    xn[k][:, cols[c]],
+                    unit[k][:, cols[c]],
+                    ACT.Identity,
+                    bias=shift[:, k : k + 1],
+                    scale=gain[:, k : k + 1],
                 )
+                for h in blocks:
+                    nc.tensor.matmul(
+                        t[h][c][:],
+                        w_sb[:, k, h * P : (h + 1) * P],
+                        xn[k][:, cols[c]],
+                        start=(k == 0),
+                        stop=(k == BLOCKS - 1),
+                    )
 
         for h, partner_factor in ((0, minus_sin), (1, sin_sb)):
             partner = 1 - h
             own = held.tile([P, N], F32, name=f"own{h}")
-            nc.vector.scalar_tensor_tensor(own[:], t[h][:], bias[:, h : h + 1], cos_sb[:], ADD, MULT)
             cross = held.tile([P, N], F32, name=f"cross{h}")
-            nc.vector.scalar_tensor_tensor(
-                cross[:], t[partner][:], bias[:, partner : partner + 1], partner_factor[:], ADD, MULT
-            )
+            for c in chunks:
+                nc.vector.scalar_tensor_tensor(
+                    own[:, cols[c]], t[h][c][:], bias[:, h : h + 1], cos_sb[:, cols[c]], ADD, MULT
+                )
+                nc.vector.scalar_tensor_tensor(
+                    cross[:, cols[c]],
+                    t[partner][c][:],
+                    bias[:, partner : partner + 1],
+                    partner_factor[:, cols[c]],
+                    ADD,
+                    MULT,
+                )
             nc.vector.tensor_tensor(window[h][:].indirect(offsets[:]), own[:], cross[:], ADD)
-            nc.sync.dma_start(out[h * P : (h + 1) * P, :], window[h][:])
+            nc.sync.dma_start(out[rows[h], :], window[h][:])

@@ -9,10 +9,12 @@ C = 256
 BLOCKS = C // P
 S = 4096
 N = 512
-CHUNKS = 2
+CHUNKS = 4
 T = N // CHUNKS
+HALVES = 2
+H = N // HALVES
 EPS = 1e-5
-WARMING_MATMULS = 6
+WARMING_MATMULS = 4
 
 FLOPS = 2 * C * C * N
 
@@ -21,7 +23,9 @@ def tile_gptj_cloud_kernel(tc, base, x, ln_w, ln_b, w, b, cos_pos, sin_pos, offs
     nc = tc.nc
     blocks = range(BLOCKS)
     chunks = range(CHUNKS)
+    halves = range(HALVES)
     cols = [slice(c * T, (c + 1) * T) for c in chunks]
+    half_cols = [slice(q * H, (q + 1) * H) for q in halves]
     rows = [slice(k * P, (k + 1) * P) for k in blocks]
     with (
         tc.tile_pool(name="held", bufs=1) as held,
@@ -29,8 +33,8 @@ def tile_gptj_cloud_kernel(tc, base, x, ln_w, ln_b, w, b, cos_pos, sin_pos, offs
     ):
         x_sb = held.tile([P, BLOCKS, N], F32, name="x_sb")
         x_blk = [x_sb[:, k, :] for k in blocks]
-        for c in chunks:
-            nc.sync.dma_start(x_sb[:, :, cols[c]], x[:, cols[c]].rearrange("(k p) n -> p k n", p=P))
+        for q in halves:
+            nc.sync.dma_start(x_sb[:, :, half_cols[q]], x[:, half_cols[q]].rearrange("(k p) n -> p k n", p=P))
 
         gain = held.tile([P, BLOCKS], F32, name="gain")
         shift = held.tile([P, BLOCKS], F32, name="shift")
@@ -47,10 +51,11 @@ def tile_gptj_cloud_kernel(tc, base, x, ln_w, ln_b, w, b, cos_pos, sin_pos, offs
         nc.sync.dma_start(w_sb[:], w.rearrange("(k p) c -> p k c", p=P))
         nc.sync.dma_start(sin_sb[:], sin_pos)
         nc.sync.dma_start(cos_sb[:], cos_pos)
-        nc.sync.dma_start(window[0][:], base[rows[0], :])
+        nc.sync.dma_start(window[0][:, 0 : S // 2], base[rows[0], 0 : S // 2])
         with nc.allow_non_contiguous_dma(reason="256 floats, one to a partition"):
             nc.sync.dma_start(bias[:], b.rearrange("(k p) o -> p (k o)", p=P))
         nc.sync.dma_start(offsets[:], offs)
+        nc.sync.dma_start(window[0][:, S // 2 : S], base[rows[0], S // 2 : S])
         nc.sync.dma_start(window[1][:], base[rows[1], :])
 
         averager = held.tile([P, P], F32, name="averager")
@@ -88,7 +93,7 @@ def tile_gptj_cloud_kernel(tc, base, x, ln_w, ln_b, w, b, cos_pos, sin_pos, offs
         rstd = held.tile([P, N], F32, name="rstd")
         unit = [held.tile([P, N], F32, name=f"unit{k}") for k in blocks]
         xn = [held.tile([P, N], BF16, name=f"xn{k}") for k in blocks]
-        t = [[psum.tile([P, T], F32, name=f"t{h}{c}") for c in chunks] for h in blocks]
+        t = [[psum.tile([P, H], F32, name=f"t{h}{q}") for q in halves] for h in blocks]
         for c in chunks:
             nc.scalar.activation(rstd[:, cols[c]], var[c][:], ACT.Abs_reciprocal_sqrt, bias=eps[:, 0:1])
             for k in blocks:
@@ -102,7 +107,7 @@ def tile_gptj_cloud_kernel(tc, base, x, ln_w, ln_b, w, b, cos_pos, sin_pos, offs
                 )
                 for h in blocks:
                     nc.tensor.matmul(
-                        t[h][c][:],
+                        t[h][c * T // H][:, c * T % H : c * T % H + T],
                         w_sb[:, k, h * P : (h + 1) * P],
                         xn[k][:, cols[c]],
                         start=(k == 0),
@@ -113,15 +118,15 @@ def tile_gptj_cloud_kernel(tc, base, x, ln_w, ln_b, w, b, cos_pos, sin_pos, offs
             partner = 1 - h
             own = held.tile([P, N], F32, name=f"own{h}")
             cross = held.tile([P, N], F32, name=f"cross{h}")
-            for c in chunks:
+            for q in halves:
                 nc.vector.scalar_tensor_tensor(
-                    own[:, cols[c]], t[h][c][:], bias[:, h : h + 1], cos_sb[:, cols[c]], ADD, MULT
+                    own[:, half_cols[q]], t[h][q][:], bias[:, h : h + 1], cos_sb[:, half_cols[q]], ADD, MULT
                 )
                 nc.vector.scalar_tensor_tensor(
-                    cross[:, cols[c]],
-                    t[partner][c][:],
+                    cross[:, half_cols[q]],
+                    t[partner][q][:],
                     bias[:, partner : partner + 1],
-                    partner_factor[:, cols[c]],
+                    partner_factor[:, half_cols[q]],
                     ADD,
                     MULT,
                 )

@@ -116,8 +116,8 @@ def tile_gptj_cloud_kernel(tc, base, x, ln_w, ln_b, w, b, cos_pos, sin_pos, offs
 
         for h, partner_factor in ((0, minus_sin), (1, sin_sb)):
             partner = 1 - h
-            own = held.tile([P, N], F32, name=f"own{h}")
-            cross = held.tile([P, N], F32, name=f"cross{h}")
+            own = held.tile([P, N], F32, name="own")
+            cross = held.tile([P, N], F32, name="cross")
             for q in halves:
                 nc.vector.scalar_tensor_tensor(
                     own[:, half_cols[q]], t[h][q][:], bias[:, h : h + 1], cos_sb[:, half_cols[q]], ADD, MULT

@@ -34,7 +34,7 @@ def tile_gptj_cloud_kernel(tc, base, x, ln_w, ln_b, w, b, cos_pos, sin_pos, offs
         x_sb = held.tile([P, BLOCKS, N], F32, name="x_sb")
         x_blk = [x_sb[:, k, :] for k in blocks]
         for q in halves:
-            nc.sync.dma_start(x_sb[:, :, half_cols[q]], x[:, half_cols[q]].rearrange("(k p) n -> p k n", p=P))
+            nc.sync.dma_start(x_sb[:, :, half_cols[q]], x[:, half_cols[q]].rearrange("(p k) n -> p k n", p=P))
 
         gain = held.tile([P, BLOCKS], F32, name="gain")
         shift = held.tile([P, BLOCKS], F32, name="shift")
@@ -45,15 +45,14 @@ def tile_gptj_cloud_kernel(tc, base, x, ln_w, ln_b, w, b, cos_pos, sin_pos, offs
         offsets = held.tile([P, N // 16], U16, name="offsets")
         window = [held.tile([P, S], F32, name=f"window{h}") for h in blocks]
 
-        with nc.allow_non_contiguous_dma(reason="256 floats, one to a partition"):
-            nc.sync.dma_start(gain[:], ln_w.rearrange("(k p) o -> p (k o)", p=P))
-            nc.sync.dma_start(shift[:], ln_b.rearrange("(k p) o -> p (k o)", p=P))
-        nc.sync.dma_start(w_sb[:], w.rearrange("(k p) c -> p k c", p=P))
+        nc.sync.dma_start(gain[:], ln_w.rearrange("(p k) o -> p (k o)", p=P))
+        nc.sync.dma_start(shift[:], ln_b.rearrange("(p k) o -> p (k o)", p=P))
+        nc.sync.dma_start(w_sb[:], w.rearrange("(p k) c -> p k c", p=P))
         nc.sync.dma_start(sin_sb[:], sin_pos)
         nc.sync.dma_start(cos_sb[:], cos_pos)
         nc.sync.dma_start(window[0][:, 0 : S // 2], base[rows[0], 0 : S // 2])
         with nc.allow_non_contiguous_dma(reason="256 floats, one to a partition"):
-            nc.sync.dma_start(bias[:], b.rearrange("(k p) o -> p (k o)", p=P))
+            nc.sync.dma_start(bias[:], b.rearrange("(h p) o -> p (h o)", p=P))
         nc.sync.dma_start(offsets[:], offs)
         nc.sync.dma_start(window[0][:, S // 2 : S], base[rows[0], S // 2 : S])
         nc.sync.dma_start(window[1][:], base[rows[1], :])

@@ -14,7 +14,6 @@ T = N // CHUNKS
 HALVES = 2
 H = N // HALVES
 EPS = 1e-5
-WARMING_MATMULS = 4
 
 FLOPS = 2 * C * C * N
 
@@ -66,11 +65,6 @@ def tile_gptj_cloud_kernel(tc, base, x, ln_w, ln_b, w, b, cos_pos, sin_pos, offs
 
         table_warmer = held.tile([P, 1], F32, name="table_warmer")
         nc.scalar.activation(table_warmer[:], eps[:], ACT.Abs_reciprocal_sqrt)
-        zeros = held.tile([P, N], BF16, name="zeros")
-        nc.gpsimd.memset(zeros[:], 0.0)
-        clock_warmer = psum.tile([P, N], F32, name="clock_warmer", tag="stat", bufs=4)
-        for i in range(WARMING_MATMULS):
-            nc.tensor.matmul(clock_warmer[:], zeros[:, 0:P], zeros[:], start=True, stop=True)
 
         x_sum = held.tile([P, N], F32, name="x_sum")
         mean = [psum.tile([P, T], F32, name=f"mean{c}", tag="stat", bufs=4) for c in chunks]

@@ -14,6 +14,7 @@ T = N // CHUNKS
 HALVES = 2
 H = N // HALVES
 EPS = 1e-5
+WARMING_MATMULS = 4
 
 FLOPS = 2 * C * C * N
 
@@ -65,6 +66,11 @@ def tile_gptj_cloud_kernel(tc, base, x, ln_w, ln_b, w, b, cos_pos, sin_pos, offs
 
         table_warmer = held.tile([P, 1], F32, name="table_warmer")
         nc.scalar.activation(table_warmer[:], eps[:], ACT.Abs_reciprocal_sqrt)
+        zeros = held.tile([P, N], BF16, name="zeros")
+        nc.gpsimd.memset(zeros[:], 0.0)
+        clock_warmer = psum.tile([P, N], F32, name="clock_warmer", tag="stat", bufs=4)
+        for i in range(WARMING_MATMULS):
+            nc.tensor.matmul(clock_warmer[:], zeros[:, 0:P], zeros[:], start=True, stop=True)
 
         x_sum = held.tile([P, N], F32, name="x_sum")
         mean = [psum.tile([P, T], F32, name=f"mean{c}", tag="stat", bufs=4) for c in chunks]
@@ -75,13 +81,13 @@ def tile_gptj_cloud_kernel(tc, base, x, ln_w, ln_b, w, b, cos_pos, sin_pos, offs
         centred = [held.tile([P, N], F32, name=f"centred{k}") for k in blocks]
         squared = [held.tile([P, N], F32, name=f"squared{k}") for k in blocks]
         var = [psum.tile([P, T], F32, name=f"var{c}", tag="stat", bufs=4) for c in chunks]
+        squared_sum = held.tile([P, N], F32, name="squared_sum")
         for c in chunks:
             for k in blocks:
                 nc.vector.tensor_tensor(centred[k][:, cols[c]], x_blk[k][:, cols[c]], mean[c][:], SUBTRACT)
                 nc.scalar.activation(squared[k][:, cols[c]], centred[k][:, cols[c]], ACT.Square)
-                nc.tensor.matmul(
-                    var[c][:], averager[:], squared[k][:, cols[c]], start=(k == 0), stop=(k == BLOCKS - 1)
-                )
+            nc.vector.tensor_tensor(squared_sum[:, cols[c]], squared[0][:, cols[c]], squared[1][:, cols[c]], ADD)
+            nc.tensor.matmul(var[c][:], averager[:], squared_sum[:, cols[c]], start=True, stop=True)
 
         rstd = held.tile([P, N], F32, name="rstd")
         unit = [held.tile([P, N], F32, name=f"unit{k}") for k in blocks]

@@ -9,11 +9,13 @@ C = 256
 BLOCKS = C // P
 S = 4096
 N = 512
-CHUNKS = 4
-T = N // CHUNKS
+EPS = 1e-5
+T = P
+CHUNKS = N // T
 HALVES = 2
 H = N // HALVES
-EPS = 1e-5
+PSUM_BANKS = 8
+STAT_BANKS = PSUM_BANKS - BLOCKS * HALVES
 WARMING_MATMULS = 4
 
 FLOPS = 2 * C * C * N
@@ -26,36 +28,36 @@ def tile_gptj_cloud_kernel(tc, base, x, ln_w, ln_b, w, b, cos_pos, sin_pos, offs
     halves = range(HALVES)
     cols = [slice(c * T, (c + 1) * T) for c in chunks]
     half_cols = [slice(q * H, (q + 1) * H) for q in halves]
-    rows = [slice(k * P, (k + 1) * P) for k in blocks]
+    half_of = [c * T // H for c in chunks]
+    cols_in_half = [slice(c * T % H, c * T % H + T) for c in chunks]
+    key_feats = [slice(h * P, (h + 1) * P) for h in blocks]
     with (
         tc.tile_pool(name="held", bufs=1) as held,
         tc.psum_pool(name="psum", bufs=1) as psum,
     ):
         x_sb = held.tile([P, BLOCKS, N], F32, name="x_sb")
-        x_blk = [x_sb[:, k, :] for k in blocks]
-        for q in halves:
-            nc.sync.dma_start(x_sb[:, :, half_cols[q]], x[:, half_cols[q]].rearrange("(p k) n -> p k n", p=P))
-
         gain = held.tile([P, BLOCKS], F32, name="gain")
         shift = held.tile([P, BLOCKS], F32, name="shift")
-        bias = held.tile([P, BLOCKS], F32, name="bias")
         w_sb = held.tile([P, BLOCKS, C], BF16, name="w_sb")
+        bias = held.tile([P, BLOCKS], F32, name="bias")
         sin_sb = held.tile([P, N], F32, name="sin_sb")
         cos_sb = held.tile([P, N], F32, name="cos_sb")
         offsets = held.tile([P, N // 16], U16, name="offsets")
         window = [held.tile([P, S], F32, name=f"window{h}") for h in blocks]
 
+        for q in halves:
+            nc.sync.dma_start(x_sb[:, :, half_cols[q]], x[:, half_cols[q]].rearrange("(p k) n -> p k n", p=P))
         nc.sync.dma_start(gain[:], ln_w.rearrange("(p k) o -> p (k o)", p=P))
         nc.sync.dma_start(shift[:], ln_b.rearrange("(p k) o -> p (k o)", p=P))
         nc.sync.dma_start(w_sb[:], w.rearrange("(p k) c -> p k c", p=P))
         nc.sync.dma_start(sin_sb[:], sin_pos)
         nc.sync.dma_start(cos_sb[:], cos_pos)
-        nc.sync.dma_start(window[0][:, 0 : S // 2], base[rows[0], 0 : S // 2])
-        with nc.allow_non_contiguous_dma(reason="256 floats, one to a partition"):
+        nc.sync.dma_start(window[0][:, 0 : S // 2], base[key_feats[0], 0 : S // 2])
+        with nc.allow_non_contiguous_dma(reason="256 floats, one to a partition and column"):
             nc.sync.dma_start(bias[:], b.rearrange("(h p) o -> p (h o)", p=P))
         nc.sync.dma_start(offsets[:], offs)
-        nc.sync.dma_start(window[0][:, S // 2 : S], base[rows[0], S // 2 : S])
-        nc.sync.dma_start(window[1][:], base[rows[1], :])
+        nc.sync.dma_start(window[0][:, S // 2 : S], base[key_feats[0], S // 2 : S])
+        nc.sync.dma_start(window[1][:], base[key_feats[1], :])
 
         averager = held.tile([P, P], F32, name="averager")
         nc.vector.memset(averager[:], 1.0 / C)
@@ -66,25 +68,23 @@ def tile_gptj_cloud_kernel(tc, base, x, ln_w, ln_b, w, b, cos_pos, sin_pos, offs
 
         table_warmer = held.tile([P, 1], F32, name="table_warmer")
         nc.scalar.activation(table_warmer[:], eps[:], ACT.Abs_reciprocal_sqrt)
-        zeros = held.tile([P, N], BF16, name="zeros")
-        nc.gpsimd.memset(zeros[:], 0.0)
-        clock_warmer = psum.tile([P, N], F32, name="clock_warmer", tag="stat", bufs=4)
+        clock_warmer = psum.tile([P, P], F32, name="clock_warmer", tag="stat", bufs=STAT_BANKS)
         for i in range(WARMING_MATMULS):
-            nc.tensor.matmul(clock_warmer[:], zeros[:, 0:P], zeros[:], start=True, stop=True)
+            nc.tensor.matmul(clock_warmer[:], averager[:], averager[:], start=True, stop=True)
 
         x_sum = held.tile([P, N], F32, name="x_sum")
-        mean = [psum.tile([P, T], F32, name=f"mean{c}", tag="stat", bufs=4) for c in chunks]
+        mean = [psum.tile([P, T], F32, name=f"mean{c}", tag="stat", bufs=STAT_BANKS) for c in chunks]
         for c in chunks:
-            nc.vector.tensor_tensor(x_sum[:, cols[c]], x_blk[0][:, cols[c]], x_blk[1][:, cols[c]], ADD)
+            nc.vector.tensor_tensor(x_sum[:, cols[c]], x_sb[:, 0, cols[c]], x_sb[:, 1, cols[c]], ADD)
             nc.tensor.matmul(mean[c][:], averager[:], x_sum[:, cols[c]], start=True, stop=True)
 
         centred = [held.tile([P, N], F32, name=f"centred{k}") for k in blocks]
         squared = [held.tile([P, N], F32, name=f"squared{k}") for k in blocks]
-        var = [psum.tile([P, T], F32, name=f"var{c}", tag="stat", bufs=4) for c in chunks]
         squared_sum = held.tile([P, N], F32, name="squared_sum")
+        var = [psum.tile([P, T], F32, name=f"var{c}", tag="stat", bufs=STAT_BANKS) for c in chunks]
         for c in chunks:
             for k in blocks:
-                nc.vector.tensor_tensor(centred[k][:, cols[c]], x_blk[k][:, cols[c]], mean[c][:], SUBTRACT)
+                nc.vector.tensor_tensor(centred[k][:, cols[c]], x_sb[:, k, cols[c]], mean[c][:], SUBTRACT)
                 nc.scalar.activation(squared[k][:, cols[c]], centred[k][:, cols[c]], ACT.Square)
             nc.vector.tensor_tensor(squared_sum[:, cols[c]], squared[0][:, cols[c]], squared[1][:, cols[c]], ADD)
             nc.tensor.matmul(var[c][:], averager[:], squared_sum[:, cols[c]], start=True, stop=True)
@@ -106,8 +106,8 @@ def tile_gptj_cloud_kernel(tc, base, x, ln_w, ln_b, w, b, cos_pos, sin_pos, offs
                 )
                 for h in blocks:
                     nc.tensor.matmul(
-                        t[h][c * T // H][:, c * T % H : c * T % H + T],
-                        w_sb[:, k, h * P : (h + 1) * P],
+                        t[h][half_of[c]][:, cols_in_half[c]],
+                        w_sb[:, k, key_feats[h]],
                         xn[k][:, cols[c]],
                         start=(k == 0),
                         stop=(k == BLOCKS - 1),
@@ -130,4 +130,4 @@ def tile_gptj_cloud_kernel(tc, base, x, ln_w, ln_b, w, b, cos_pos, sin_pos, offs
                     MULT,
                 )
             nc.vector.tensor_tensor(window[h][:].indirect(offsets[:]), own[:], cross[:], ADD)
-            nc.sync.dma_start(out[rows[h], :], window[h][:])
+            nc.sync.dma_start(out[key_feats[h], :], window[h][:])

@@ -63,8 +63,6 @@ def tile_gptj_cloud_kernel(tc, base, x, ln_w, ln_b, w, b, cos_pos, sin_pos, offs
         nc.vector.memset(averager[:], 1.0 / C)
         eps = held.tile([P, 1], F32, name="eps")
         nc.vector.memset(eps[:], EPS)
-        minus_sin = held.tile([P, N], F32, name="minus_sin")
-        nc.gpsimd.tensor_scalar(minus_sin[:], sin_sb[:], -1.0, 0.0, MULT, ADD)
 
         table_warmer = held.tile([P, 1], F32, name="table_warmer")
         nc.scalar.activation(table_warmer[:], eps[:], ACT.Abs_reciprocal_sqrt)
@@ -113,6 +111,8 @@ def tile_gptj_cloud_kernel(tc, base, x, ln_w, ln_b, w, b, cos_pos, sin_pos, offs
                         stop=(k == BLOCKS - 1),
                     )
 
+        minus_sin = held.tile([P, N], F32, name="minus_sin")
+        nc.vector.tensor_scalar_mul(minus_sin[:], sin_sb[:], -1.0)
         for h, partner_factor in ((0, minus_sin), (1, sin_sb)):
             partner = 1 - h
             own = held.tile([P, N], F32, name="own")

@@ -1,4 +1,5 @@
 import concourse.mybir as mybir
+from concourse.masks import make_identity
 
 F32, BF16, U16 = mybir.dt.float32, mybir.dt.bfloat16, mybir.dt.uint16
 ADD, SUBTRACT, MULT = mybir.AluOpType.add, mybir.AluOpType.subtract, mybir.AluOpType.mult
@@ -15,7 +16,7 @@ CHUNKS = N // T
 HALVES = 2
 H = N // HALVES
 PSUM_BANKS = 8
-STAT_BANKS = PSUM_BANKS - BLOCKS * HALVES
+BN_STATS = 6
 WARMING_MATMULS = 4
 
 FLOPS = 2 * C * C * N
@@ -59,45 +60,45 @@ def tile_gptj_cloud_kernel(tc, base, x, ln_w, ln_b, w, b, cos_pos, sin_pos, offs
         nc.sync.dma_start(window[0][:, S // 2 : S], base[key_feats[0], S // 2 : S])
         nc.sync.dma_start(window[1][:], base[key_feats[1], :])
 
-        averager = held.tile([P, P], F32, name="averager")
-        nc.vector.memset(averager[:], 1.0 / C)
+        identity = held.tile([P, P], F32, name="identity")
+        make_identity(nc, identity[:])
         eps = held.tile([P, 1], F32, name="eps")
         nc.vector.memset(eps[:], EPS)
+        warmth = held.tile([P, P], F32, name="warmth")
+        nc.vector.memset(warmth[:], 0.0)
 
         table_warmer = held.tile([P, 1], F32, name="table_warmer")
         nc.scalar.activation(table_warmer[:], eps[:], ACT.Abs_reciprocal_sqrt)
-        clock_warmer = psum.tile([P, P], F32, name="clock_warmer", tag="stat", bufs=STAT_BANKS)
+        clock_warmer = psum.tile([P, P], F32, name="clock_warmer", tag="bank", bufs=PSUM_BANKS)
         for i in range(WARMING_MATMULS):
-            nc.tensor.matmul(clock_warmer[:], averager[:], averager[:], start=True, stop=True)
+            nc.tensor.matmul(clock_warmer[:], warmth[:], warmth[:], start=True, stop=True)
 
-        x_sum = held.tile([P, N], F32, name="x_sum")
-        mean = [psum.tile([P, T], F32, name=f"mean{c}", tag="stat", bufs=STAT_BANKS) for c in chunks]
-        for c in chunks:
-            nc.vector.tensor_tensor(x_sum[:, cols[c]], x_sb[:, 0, cols[c]], x_sb[:, 1, cols[c]], ADD)
-            nc.tensor.matmul(mean[c][:], averager[:], x_sum[:, cols[c]], start=True, stop=True)
-
-        centred = [held.tile([P, N], F32, name=f"centred{k}") for k in blocks]
-        squared = [held.tile([P, N], F32, name=f"squared{k}") for k in blocks]
-        squared_sum = held.tile([P, N], F32, name="squared_sum")
-        var = [psum.tile([P, T], F32, name=f"var{c}", tag="stat", bufs=STAT_BANKS) for c in chunks]
+        stats = held.tile([P, CHUNKS, BN_STATS], F32, name="stats")
+        moments = held.tile([P, CHUNKS, 2], F32, name="moments")
+        rstd = held.tile([P, CHUNKS], F32, name="rstd")
+        unit = held.tile([P, CHUNKS, C], F32, name="unit")
+        x_turned = [psum.tile([P, C], F32, name=f"x_turned{c}", tag="bank", bufs=PSUM_BANKS) for c in chunks]
+        unit_back = [psum.tile([P, BLOCKS, T], F32, name=f"unit_back{c}", tag="bank", bufs=PSUM_BANKS) for c in chunks]
         for c in chunks:
             for k in blocks:
-                nc.vector.tensor_tensor(centred[k][:, cols[c]], x_sb[:, k, cols[c]], mean[c][:], SUBTRACT)
-                nc.scalar.activation(squared[k][:, cols[c]], centred[k][:, cols[c]], ACT.Square)
-            nc.vector.tensor_tensor(squared_sum[:, cols[c]], squared[0][:, cols[c]], squared[1][:, cols[c]], ADD)
-            nc.tensor.matmul(var[c][:], averager[:], squared_sum[:, cols[c]], start=True, stop=True)
+                nc.tensor.transpose(x_turned[c][:, key_feats[k]], x_sb[:, k, cols[c]], identity[:])
+            nc.vector.bn_stats(stats[:, c, :], x_turned[c][:])
+            nc.vector.bn_aggr(moments[:, c, :], stats[:, c, :])
+            nc.scalar.activation(rstd[:, c : c + 1], moments[:, c, 1:2], ACT.Abs_reciprocal_sqrt, bias=eps[:, 0:1])
+            nc.vector.tensor_scalar(
+                unit[:, c, :], x_turned[c][:], moments[:, c, 0:1], rstd[:, c : c + 1], op0=SUBTRACT, op1=MULT
+            )
+        for c in chunks:
+            for k in blocks:
+                nc.tensor.transpose(unit_back[c][:, k, :], unit[:, c, key_feats[k]], identity[:])
 
-        rstd = held.tile([P, N], F32, name="rstd")
-        unit = [held.tile([P, N], F32, name=f"unit{k}") for k in blocks]
         xn = [held.tile([P, N], BF16, name=f"xn{k}") for k in blocks]
-        t = [[psum.tile([P, H], F32, name=f"t{h}{q}") for q in halves] for h in blocks]
+        t = [[psum.tile([P, H], F32, name=f"t{h}{q}", tag="bank", bufs=PSUM_BANKS) for q in halves] for h in blocks]
         for c in chunks:
-            nc.scalar.activation(rstd[:, cols[c]], var[c][:], ACT.Abs_reciprocal_sqrt, bias=eps[:, 0:1])
             for k in blocks:
-                nc.vector.tensor_tensor(unit[k][:, cols[c]], centred[k][:, cols[c]], rstd[:, cols[c]], MULT)
                 nc.scalar.activation(
                     xn[k][:, cols[c]],
-                    unit[k][:, cols[c]],
+                    unit_back[c][:, k, :],
                     ACT.Identity,
                     bias=shift[:, k : k + 1],
                     scale=gain[:, k : k + 1],
@@ -112,7 +113,7 @@ def tile_gptj_cloud_kernel(tc, base, x, ln_w, ln_b, w, b, cos_pos, sin_pos, offs
                     )
 
         minus_sin = held.tile([P, N], F32, name="minus_sin")
-        nc.vector.tensor_scalar_mul(minus_sin[:], sin_sb[:], -1.0)
+        nc.gpsimd.tensor_scalar_mul(minus_sin[:], sin_sb[:], -1.0)
         for h, partner_factor in ((0, minus_sin), (1, sin_sb)):
             partner = 1 - h
             own = held.tile([P, N], F32, name="own")

@@ -18,6 +18,9 @@ H = N // HALVES
 PSUM_BANKS = 8
 BN_STATS = 6
 WARMING_MATMULS = 4
+VECTORS = 3
+COLUMNS = VECTORS * BLOCKS
+ROWS = 32
 
 FLOPS = 2 * C * C * N
 
@@ -37,25 +40,22 @@ def tile_gptj_cloud_kernel(tc, base, x, ln_w, ln_b, w, b, cos_pos, sin_pos, offs
         tc.psum_pool(name="psum", bufs=1) as psum,
     ):
         x_sb = held.tile([P, BLOCKS, N], F32, name="x_sb")
-        gain = held.tile([P, BLOCKS], F32, name="gain")
-        shift = held.tile([P, BLOCKS], F32, name="shift")
         w_sb = held.tile([P, BLOCKS, C], BF16, name="w_sb")
-        bias = held.tile([P, BLOCKS], F32, name="bias")
+        rows = held.tile([ROWS, P], F32, name="rows")
         sin_sb = held.tile([P, N], F32, name="sin_sb")
         cos_sb = held.tile([P, N], F32, name="cos_sb")
         offsets = held.tile([P, N // 16], U16, name="offsets")
         window = [held.tile([P, S], F32, name=f"window{h}") for h in blocks]
 
+        nc.vector.memset(rows[:], 0.0)
         for q in halves:
-            nc.sync.dma_start(x_sb[:, :, half_cols[q]], x[:, half_cols[q]].rearrange("(p k) n -> p k n", p=P))
-        nc.sync.dma_start(gain[:], ln_w.rearrange("(p k) o -> p (k o)", p=P))
-        nc.sync.dma_start(shift[:], ln_b.rearrange("(p k) o -> p (k o)", p=P))
-        nc.sync.dma_start(w_sb[:], w.rearrange("(p k) c -> p k c", p=P))
+            nc.sync.dma_start(x_sb[:, :, half_cols[q]], x[:, half_cols[q]].rearrange("(k p) n -> p k n", p=P))
+        for i, vector in enumerate((ln_w, ln_b, b)):
+            nc.sync.dma_start(rows[i * BLOCKS : (i + 1) * BLOCKS, :], vector.rearrange("(k p) o -> k (p o)", p=P))
+        nc.sync.dma_start(w_sb[:], w.rearrange("(k p) c -> p k c", p=P))
         nc.sync.dma_start(sin_sb[:], sin_pos)
-        nc.sync.dma_start(cos_sb[:], cos_pos)
         nc.sync.dma_start(window[0][:, 0 : S // 2], base[key_feats[0], 0 : S // 2])
-        with nc.allow_non_contiguous_dma(reason="256 floats, one to a partition and column"):
-            nc.sync.dma_start(bias[:], b.rearrange("(h p) o -> p (h o)", p=P))
+        nc.sync.dma_start(cos_sb[:], cos_pos)
         nc.sync.dma_start(offsets[:], offs)
         nc.sync.dma_start(window[0][:, S // 2 : S], base[key_feats[0], S // 2 : S])
         nc.sync.dma_start(window[1][:], base[key_feats[1], :])
@@ -88,6 +88,12 @@ def tile_gptj_cloud_kernel(tc, base, x, ln_w, ln_b, w, b, cos_pos, sin_pos, offs
             nc.vector.tensor_scalar(
                 unit[:, c, :], x_turned[c][:], moments[:, c, 0:1], rstd[:, c : c + 1], op0=SUBTRACT, op1=MULT
             )
+        turned = psum.tile([P, COLUMNS], F32, name="turned", tag="bank", bufs=PSUM_BANKS)
+        nc.tensor.matmul(turned[:], rows[:], identity[0:ROWS, 0:COLUMNS], start=True, stop=True)
+        columns = held.tile([P, COLUMNS], F32, name="columns")
+        nc.scalar.copy(columns[:], turned[:])
+        gain, shift, bias = [columns[:, i * BLOCKS : (i + 1) * BLOCKS] for i in range(VECTORS)]
+
         for c in chunks:
             for k in blocks:
                 nc.tensor.transpose(unit_back[c][:, k, :], unit[:, c, key_feats[k]], identity[:])

@@ -122,7 +122,7 @@ def tile_gptj_cloud_kernel(tc, base, x, ln_w, ln_b, w, b, cos_pos, sin_pos, offs
         nc.gpsimd.tensor_scalar_mul(minus_sin[:], sin_sb[:], -1.0)
         for h, partner_factor in ((0, minus_sin), (1, sin_sb)):
             partner = 1 - h
-            own = held.tile([P, N], F32, name="own")
+            own = held.tile([P, N], F32, name=f"own{h}")
             cross = held.tile([P, N], F32, name="cross")
             for q in halves:
                 nc.vector.scalar_tensor_tensor(

@@ -17,7 +17,8 @@ HALVES = 2
 H = N // HALVES
 PSUM_BANKS = 8
 BN_STATS = 6
-WARMING_MATMULS = 4
+EARLY_WARMING = 4
+LATE_WARMING = 2
 VECTORS = 3
 COLUMNS = VECTORS * BLOCKS
 ROWS = 32
@@ -70,7 +71,7 @@ def tile_gptj_cloud_kernel(tc, base, x, ln_w, ln_b, w, b, cos_pos, sin_pos, offs
         table_warmer = held.tile([P, 1], F32, name="table_warmer")
         nc.scalar.activation(table_warmer[:], eps[:], ACT.Abs_reciprocal_sqrt)
         clock_warmer = psum.tile([P, P], F32, name="clock_warmer", tag="bank", bufs=PSUM_BANKS)
-        for i in range(WARMING_MATMULS):
+        for i in range(EARLY_WARMING):
             nc.tensor.matmul(clock_warmer[:], warmth[:], warmth[:], start=True, stop=True)
 
         stats = held.tile([P, CHUNKS, BN_STATS], F32, name="stats")
@@ -88,6 +89,9 @@ def tile_gptj_cloud_kernel(tc, base, x, ln_w, ln_b, w, b, cos_pos, sin_pos, offs
             nc.vector.tensor_scalar(
                 unit[:, c, :], x_turned[c][:], moments[:, c, 0:1], rstd[:, c : c + 1], op0=SUBTRACT, op1=MULT
             )
+        for i in range(LATE_WARMING):
+            nc.tensor.matmul(clock_warmer[:], warmth[:], warmth[:], start=True, stop=True)
+
         turned = psum.tile([P, COLUMNS], F32, name="turned", tag="bank", bufs=PSUM_BANKS)
         nc.tensor.matmul(turned[:], rows[:], identity[0:ROWS, 0:COLUMNS], start=True, stop=True)
         columns = held.tile([P, COLUMNS], F32, name="columns")

@@ -17,8 +17,7 @@ HALVES = 2
 H = N // HALVES
 PSUM_BANKS = 8
 BN_STATS = 6
-EARLY_WARMING = 4
-LATE_WARMING = 2
+EARLY_WARMING = 3
 VECTORS = 3
 COLUMNS = VECTORS * BLOCKS
 ROWS = 32
@@ -55,8 +54,8 @@ def tile_gptj_cloud_kernel(tc, base, x, ln_w, ln_b, w, b, cos_pos, sin_pos, offs
             nc.sync.dma_start(rows[i * BLOCKS : (i + 1) * BLOCKS, :], vector.rearrange("(k p) o -> k (p o)", p=P))
         nc.sync.dma_start(w_sb[:], w.rearrange("(k p) c -> p k c", p=P))
         nc.sync.dma_start(sin_sb[:], sin_pos)
-        nc.sync.dma_start(window[0][:, 0 : S // 2], base[key_feats[0], 0 : S // 2])
         nc.sync.dma_start(cos_sb[:], cos_pos)
+        nc.sync.dma_start(window[0][:, 0 : S // 2], base[key_feats[0], 0 : S // 2])
         nc.sync.dma_start(offsets[:], offs)
         nc.sync.dma_start(window[0][:, S // 2 : S], base[key_feats[0], S // 2 : S])
         nc.sync.dma_start(window[1][:], base[key_feats[1], :])
@@ -89,8 +88,8 @@ def tile_gptj_cloud_kernel(tc, base, x, ln_w, ln_b, w, b, cos_pos, sin_pos, offs
             nc.vector.tensor_scalar(
                 unit[:, c, :], x_turned[c][:], moments[:, c, 0:1], rstd[:, c : c + 1], op0=SUBTRACT, op1=MULT
             )
-        for i in range(LATE_WARMING):
-            nc.tensor.matmul(clock_warmer[:], warmth[:], warmth[:], start=True, stop=True)
+        for k in blocks:
+            nc.tensor.matmul(clock_warmer[:], identity[:], x_sb[:, k, cols[-1]], start=True, stop=True)
 
         turned = psum.tile([P, COLUMNS], F32, name="turned", tag="bank", bufs=PSUM_BANKS)
         nc.tensor.matmul(turned[:], rows[:], identity[0:ROWS, 0:COLUMNS], start=True, stop=True)

@@ -55,10 +55,9 @@ def tile_gptj_cloud_kernel(tc, base, x, ln_w, ln_b, w, b, cos_pos, sin_pos, offs
         nc.sync.dma_start(w_sb[:], w.rearrange("(k p) c -> p k c", p=P))
         nc.sync.dma_start(sin_sb[:], sin_pos)
         nc.sync.dma_start(cos_sb[:], cos_pos)
-        nc.sync.dma_start(window[0][:, 0 : S // 2], base[key_feats[0], 0 : S // 2])
         nc.sync.dma_start(offsets[:], offs)
-        nc.sync.dma_start(window[0][:, S // 2 : S], base[key_feats[0], S // 2 : S])
-        nc.sync.dma_start(window[1][:], base[key_feats[1], :])
+        for h in blocks:
+            nc.sync.dma_start(window[h][:], base[key_feats[h], :])
 
         identity = held.tile([P, P], F32, name="identity")
         make_identity(nc, identity[:])

import concourse.mybir as mybir
from concourse.masks import make_identity

F32, BF16, U16 = mybir.dt.float32, mybir.dt.bfloat16, mybir.dt.uint16
ADD, SUBTRACT, MULT = mybir.AluOpType.add, mybir.AluOpType.subtract, mybir.AluOpType.mult
ACT = mybir.ActivationFunctionType

P = 128
C = 256
BLOCKS = C // P
S = 4096
N = 512
EPS = 1e-5
T = P
CHUNKS = N // T
HALVES = 2
H = N // HALVES
PSUM_BANKS = 8
BN_STATS = 6
EARLY_WARMING = 3
VECTORS = 3
COLUMNS = VECTORS * BLOCKS
ROWS = 32

FLOPS = 2 * C * C * N


def tile_gptj_cloud_kernel(tc, base, x, ln_w, ln_b, w, b, cos_pos, sin_pos, offs, out):
    nc = tc.nc
    blocks = range(BLOCKS)
    chunks = range(CHUNKS)
    halves = range(HALVES)
    cols = [slice(c * T, (c + 1) * T) for c in chunks]
    half_cols = [slice(q * H, (q + 1) * H) for q in halves]
    half_of = [c * T // H for c in chunks]
    cols_in_half = [slice(c * T % H, c * T % H + T) for c in chunks]
    key_feats = [slice(h * P, (h + 1) * P) for h in blocks]
    with (
        tc.tile_pool(name="held", bufs=1) as held,
        tc.psum_pool(name="psum", bufs=1) as psum,
    ):
        x_sb = held.tile([P, BLOCKS, N], F32, name="x_sb")
        w_sb = held.tile([P, BLOCKS, C], BF16, name="w_sb")
        rows = held.tile([ROWS, P], F32, name="rows")
        sin_sb = held.tile([P, N], F32, name="sin_sb")
        cos_sb = held.tile([P, N], F32, name="cos_sb")
        offsets = held.tile([P, N // 16], U16, name="offsets")
        window = [held.tile([P, S], F32, name=f"window{h}") for h in blocks]

        nc.vector.memset(rows[:], 0.0)
        for q in halves:
            nc.sync.dma_start(x_sb[:, :, half_cols[q]], x[:, half_cols[q]].rearrange("(k p) n -> p k n", p=P))
        for i, vector in enumerate((ln_w, ln_b, b)):
            nc.sync.dma_start(rows[i * BLOCKS : (i + 1) * BLOCKS, :], vector.rearrange("(k p) o -> k (p o)", p=P))
        nc.sync.dma_start(w_sb[:], w.rearrange("(k p) c -> p k c", p=P))
        nc.sync.dma_start(sin_sb[:], sin_pos)
        nc.sync.dma_start(cos_sb[:], cos_pos)
        nc.sync.dma_start(offsets[:], offs)
        for h in blocks:
            nc.sync.dma_start(window[h][:], base[key_feats[h], :])

        identity = held.tile([P, P], F32, name="identity")
        make_identity(nc, identity[:])
        eps = held.tile([P, 1], F32, name="eps")
        nc.vector.memset(eps[:], EPS)
        warmth = held.tile([P, P], F32, name="warmth")
        nc.vector.memset(warmth[:], 0.0)

        table_warmer = held.tile([P, 1], F32, name="table_warmer")
        nc.scalar.activation(table_warmer[:], eps[:], ACT.Abs_reciprocal_sqrt)
        clock_warmer = psum.tile([P, P], F32, name="clock_warmer", tag="bank", bufs=PSUM_BANKS)
        for i in range(EARLY_WARMING):
            nc.tensor.matmul(clock_warmer[:], warmth[:], warmth[:], start=True, stop=True)

        stats = held.tile([P, CHUNKS, BN_STATS], F32, name="stats")
        moments = held.tile([P, CHUNKS, 2], F32, name="moments")
        rstd = held.tile([P, CHUNKS], F32, name="rstd")
        unit = held.tile([P, CHUNKS, C], F32, name="unit")
        x_turned = [psum.tile([P, C], F32, name=f"x_turned{c}", tag="bank", bufs=PSUM_BANKS) for c in chunks]
        unit_back = [psum.tile([P, BLOCKS, T], F32, name=f"unit_back{c}", tag="bank", bufs=PSUM_BANKS) for c in chunks]
        for c in chunks:
            for k in blocks:
                nc.tensor.transpose(x_turned[c][:, key_feats[k]], x_sb[:, k, cols[c]], identity[:])
            nc.vector.bn_stats(stats[:, c, :], x_turned[c][:])
            nc.vector.bn_aggr(moments[:, c, :], stats[:, c, :])
            nc.scalar.activation(rstd[:, c : c + 1], moments[:, c, 1:2], ACT.Abs_reciprocal_sqrt, bias=eps[:, 0:1])
            nc.vector.tensor_scalar(
                unit[:, c, :], x_turned[c][:], moments[:, c, 0:1], rstd[:, c : c + 1], op0=SUBTRACT, op1=MULT
            )
        for k in blocks:
            nc.tensor.matmul(clock_warmer[:], identity[:], x_sb[:, k, cols[-1]], start=True, stop=True)

        turned = psum.tile([P, COLUMNS], F32, name="turned", tag="bank", bufs=PSUM_BANKS)
        nc.tensor.matmul(turned[:], rows[:], identity[0:ROWS, 0:COLUMNS], start=True, stop=True)
        columns = held.tile([P, COLUMNS], F32, name="columns")
        nc.scalar.copy(columns[:], turned[:])
        gain, shift, bias = [columns[:, i * BLOCKS : (i + 1) * BLOCKS] for i in range(VECTORS)]

        for c in chunks:
            for k in blocks:
                nc.tensor.transpose(unit_back[c][:, k, :], unit[:, c, key_feats[k]], identity[:])

        xn = [held.tile([P, N], BF16, name=f"xn{k}") for k in blocks]
        t = [[psum.tile([P, H], F32, name=f"t{h}{q}", tag="bank", bufs=PSUM_BANKS) for q in halves] for h in blocks]
        for c in chunks:
            for k in blocks:
                nc.scalar.activation(
                    xn[k][:, cols[c]],
                    unit_back[c][:, k, :],
                    ACT.Identity,
                    bias=shift[:, k : k + 1],
                    scale=gain[:, k : k + 1],
                )
                for h in blocks:
                    nc.tensor.matmul(
                        t[h][half_of[c]][:, cols_in_half[c]],
                        w_sb[:, k, key_feats[h]],
                        xn[k][:, cols[c]],
                        start=(k == 0),
                        stop=(k == BLOCKS - 1),
                    )

        minus_sin = held.tile([P, N], F32, name="minus_sin")
        nc.gpsimd.tensor_scalar_mul(minus_sin[:], sin_sb[:], -1.0)
        for h, partner_factor in ((0, minus_sin), (1, sin_sb)):
            partner = 1 - h
            own = held.tile([P, N], F32, name=f"own{h}")
            cross = held.tile([P, N], F32, name="cross")
            for q in halves:
                nc.vector.scalar_tensor_tensor(
                    own[:, half_cols[q]], t[h][q][:], bias[:, h : h + 1], cos_sb[:, half_cols[q]], ADD, MULT
                )
                nc.vector.scalar_tensor_tensor(
                    cross[:, half_cols[q]],
                    t[partner][q][:],
                    bias[:, partner : partner + 1],
                    partner_factor[:, half_cols[q]],
                    ADD,
                    MULT,
                )
            nc.vector.tensor_tensor(window[h][:].indirect(offsets[:]), own[:], cross[:], ADD)
            nc.sync.dma_start(out[key_feats[h], :], window[h][:])
